import numpy as np
import ml_dtypes


def mxq(x, axis, fmt="e4m3"):
    dtype, down = {"e4m3": (ml_dtypes.float8_e4m3fn, 7), "e5m2": (ml_dtypes.float8_e5m2, 14)}[fmt]
    v = np.moveaxis(np.asarray(x, np.float32).astype(ml_dtypes.bfloat16).astype(np.float64), axis, -1)
    blocks = v.reshape(v.shape[:-1] + (-1, 32))
    amax = np.abs(blocks).max(-1, keepdims=True)
    byte = np.maximum(np.where(amax > 0, np.frexp(amax)[1] - 1 + 127, 0) - down, 1)
    scale = np.exp2(byte - 127.0)
    codes = (blocks / scale).astype(np.float32).astype(dtype).astype(np.float64)
    return np.moveaxis((codes * scale).reshape(v.shape), -1, axis)


WIDE = False


def mx_kscale(k):
    if not WIDE:
        return np.ones(k)
    levels = np.array([10, -10, 5, -5, 0])
    if k % 512:
        return np.exp2(np.random.permutation(np.resize(levels, k // 32))).repeat(32)
    a = np.empty((k // 512, 16))
    for p in range(k // 512):
        a[p, :8] = np.random.permutation(np.resize(levels, 8))
        for g in range(8):
            far = levels[np.abs(levels - a[p, g]) >= 10]
            a[p, g + 8] = far[np.random.randint(len(far))]
    return np.exp2(a.ravel()).repeat(32)


BF16 = ml_dtypes.bfloat16


def bf(x):
    return np.asarray(x, np.float32).astype(BF16)


def f64(x):
    return np.asarray(x).astype(np.float64)


B, H, N, D, DT, NH = 32, 128, 128, 1024, 1024, 8


def softmax(v, axis):
    e = np.exp(v - v.max(axis=axis, keepdims=True))
    return e / e.sum(axis=axis, keepdims=True)


def setup_inputs():
    s = mx_kscale(DT)
    return {"cand_topics": bf(np.random.standard_normal((B, N, DT)) * s),
            "Wq": bf(np.random.standard_normal((D, DT)) * 2.0 / np.sqrt(DT) / s[None, :]),
            "bq": bf(np.random.standard_normal(D) * 0.5)}


def reference(cand_topics, Wq, bq):
    q = (mxq(f64(cand_topics), 2, "e4m3") @ mxq(f64(Wq), 1, "e4m3").T) + f64(bq)
    query_weights = softmax(np.sqrt((q ** 2).sum(axis=-1)), 1)
    return q, query_weights

@@ -1,0 +1,257 @@
+from contextlib import ExitStack
+
+import concourse.mybir as mybir
+from concourse.masks import make_identity
+
+F32 = mybir.dt.float32
+BF16 = mybir.dt.bfloat16
+U32 = mybir.dt.uint32
+U8 = mybir.dt.uint8
+FP8X4 = mybir.dt.float8_e4m3fn_x4
+ACT = mybir.ActivationFunctionType
+ALU = mybir.AluOpType
+AXIS = mybir.AxisListType
+
+P = 128
+PACK = 4
+USERS = 32
+CANDIDATES = 128
+ROWS = USERS * CANDIDATES
+K = 1024
+FEATURES = 1024
+PASSES = K // (P * PACK)
+BLOCKS = K // 2 // P
+BANK = 512
+HALVES = FEATURES // BANK
+TILES = ROWS // P
+GROUP = 2
+GROUPS = TILES // GROUP
+VECTOR_SHARE = 4
+W_BLOCKS = 2
+W_CHUNK = W_BLOCKS * P
+W_CHUNKS = FEATURES // W_CHUNK
+PER_USER = CANDIDATES // TILES
+
+FLOPS = 2 * ROWS * K * FEATURES
+
+
+def tile_candidateaware_clickednewsattention_pa_t_kernel(
+    tc, cand_topics, Wq, bq, out_0, out_1
+):
+    nc = tc.nc
+    x_rows = cand_topics.flatten_outer_dims().rearrange("(p t) k -> p t k", t=TILES)
+    q_rows = out_0.flatten_outer_dims().rearrange("(p t) d -> p t d", t=TILES)
+    w_rows = Wq.rearrange("(c p) k -> p c k", p=P)
+
+    with ExitStack() as stack:
+        const = stack.enter_context(tc.tile_pool(name="const", bufs=1))
+        raw = stack.enter_context(tc.tile_pool(name="raw", bufs=1))
+        packed = stack.enter_context(tc.tile_pool(name="packed", bufs=2))
+        results = stack.enter_context(tc.tile_pool(name="results", bufs=6))
+        scrap = stack.enter_context(tc.tile_pool(name="scrap", bufs=4))
+        flipped = stack.enter_context(tc.psum_pool(name="flipped", bufs=4))
+        sums = stack.enter_context(tc.psum_pool(name="sums", bufs=4))
+        stack.enter_context(tc.manual_schedule())
+
+        bias_rows = const.tile([P, FEATURES], BF16)
+        nc.vector.memset(bias_rows[:], 0.0)
+
+        w_raw = [
+            raw.tile([P, W_BLOCKS, K], BF16, name="w_raw%d" % c) for c in range(W_CHUNKS)
+        ]
+        x_raw = [raw.tile([P, GROUP, K], BF16, name="x_raw%d" % i) for i in range(GROUPS)]
+
+        def load_w(c):
+            nc.sync.dma_start(
+                out=w_raw[c][:], in_=w_rows[:, c * W_BLOCKS : (c + 1) * W_BLOCKS, :]
+            )
+
+        def load_x(i):
+            nc.sync.dma_start(out=x_raw[i][:], in_=x_rows[:, i * GROUP : (i + 1) * GROUP, :])
+
+        load_w(0)
+        load_x(0)
+        nc.sync.dma_start(out=bias_rows[0:1, :], in_=bq.unsqueeze(0))
+        for c in range(1, W_CHUNKS):
+            load_w(c)
+        for i in range(1, GROUPS):
+            load_x(i)
+
+        one = const.tile([P, 1], F32)
+        nc.vector.memset(one[:], 1.0)
+        warm_sqrt = const.tile([P, 1], F32)
+        nc.scalar.activation(out=warm_sqrt[:], in_=one[:], func=ACT.Sqrt)
+
+        ident = const.tile([P, P], F32)
+        make_identity(nc, ident[:])
+
+        pick = const.tile([P, PER_USER, P], F32)
+        nc.vector.memset(pick[:], 0.0)
+        nc.vector.tensor_copy(
+            out=pick[:, :, 0:USERS], in_=ident[:].rearrange("p (b j) -> p j b", j=PER_USER)
+        )
+
+        ones = const.tile([P, P], BF16)
+        nc.vector.memset(ones[:], 1.0)
+        bias = const.tile([P, FEATURES], F32)
+
+        def spread_bias():
+            for h in range(HALVES):
+                cols = slice(h * BANK, (h + 1) * BANK)
+                spread = sums.tile([P, BANK], F32, tag="sum")
+                nc.tensor.matmul(
+                    out=spread[:], lhsT=ones[:], rhs=bias_rows[:, cols], start=True, stop=True
+                )
+                nc.scalar.copy(out=bias[:, cols], in_=spread[:])
+
+        def flip(words, grouped_words, on_vector):
+            bank = flipped.tile([P, BLOCKS, P], F32, tag="flip")
+            for g in range(PASSES):
+                for u in range(2):
+                    nc.tensor.transpose(
+                        out=bank[:, 2 * g + u, :],
+                        in_=words[:, 2 * P * g + u : 2 * P * (g + 1) : 2],
+                        identity=ident[:],
+                    )
+            planes = bank[:].rearrange("p (g u) r -> p g r u", u=2)
+            if on_vector:
+                nc.vector.tensor_copy(out=grouped_words, in_=planes)
+            else:
+                nc.scalar.copy(out=grouped_words, in_=planes)
+
+        w_grouped = const.tile([P, PASSES, FEATURES, PACK], BF16, align_bytes=64)
+        w_codes = const.tile([P, PASSES, FEATURES], U32, align_bytes=64)
+        w_scales = const.tile([P, PASSES, FEATURES], U8, align_bytes=64)
+
+        def flip_w(c):
+            for b in range(W_BLOCKS):
+                first = c * W_CHUNK + b * P
+                flip(
+                    w_raw[c][:].bitcast(F32)[:, b, :],
+                    w_grouped[:].bitcast(F32)[:, :, first : first + P, :],
+                    on_vector=(b == 0),
+                )
+
+        def quantise_w(c):
+            cols = slice(c * W_CHUNK, (c + 1) * W_CHUNK)
+            for g in range(PASSES):
+                nc.vector.quantize_mx(
+                    out=w_codes[:, g, cols].bitcast(FP8X4),
+                    scales=w_scales[:, g, cols],
+                    in_=w_grouped[:, g, cols, :].rearrange("p d e -> p (d e)"),
+                )
+
+        x_grouped = {}
+        x_codes = {}
+        x_scales = {}
+
+        def flip_x(i):
+            x_grouped[i] = packed.tile(
+                [P, GROUP, PASSES, P, PACK], BF16, align_bytes=64, name="x_grouped", tag="xg"
+            )
+            for j in range(GROUP):
+                flip(
+                    x_raw[i][:].bitcast(F32)[:, j, :],
+                    x_grouped[i][:].bitcast(F32)[:, j],
+                    on_vector=((i * GROUP + j) % VECTOR_SHARE == 0),
+                )
+
+        def quantise_x(i):
+            x_codes[i] = packed.tile(
+                [P, GROUP, PASSES, P], U32, align_bytes=64, name="x_codes", tag="xc"
+            )
+            x_scales[i] = packed.tile(
+                [P, GROUP, PASSES, P], U8, align_bytes=64, name="x_scales", tag="xs"
+            )
+            nc.vector.quantize_mx(
+                out=x_codes[i][:].rearrange("p j g r -> p (j g r)").bitcast(FP8X4),
+                scales=x_scales[i][:].rearrange("p j g r -> p (j g r)"),
+                in_=x_grouped[i][:].rearrange("p j g r e -> p (j g r e)"),
+            )
+
+        square_sums = const.tile([P, TILES], F32)
+
+        q_group = {}
+
+        def multiply(i, j):
+            t = i * GROUP + j
+            if j == 0:
+                q_group[i] = results.tile([P, GROUP, FEATURES], F32, name="q", tag="q")
+            q = q_group[i]
+            for h in range(HALVES):
+                cols = slice(h * BANK, (h + 1) * BANK)
+                acc = sums.tile([P, BANK], F32, tag="sum")
+                for g in range(PASSES):
+                    nc.tensor.matmul_mx(
+                        out=acc[:],
+                        lhsT=x_codes[i][:, j, g, :].bitcast(FP8X4),
+                        lhsT_scale=x_scales[i][:, j, g, :],
+                        rhs=w_codes[:, g, cols].bitcast(FP8X4),
+                        rhs_scale=w_scales[:, g, cols],
+                        start=(g == 0),
+                        stop=(g == PASSES - 1),
+                    )
+                nc.vector.tensor_tensor(
+                    out=q[:, j, cols], in0=acc[:], in1=bias[:, cols], op=ALU.add
+                )
+            squares = scrap.tile([P, FEATURES], BF16, tag="squares")
+            nc.scalar.activation(
+                out=squares[:],
+                in_=q[:, j, :],
+                func=ACT.Square,
+                accum_out=square_sums[:, t : t + 1],
+            )
+            if j == GROUP - 1:
+                nc.sync.dma_start(out=q_rows[:, i * GROUP : (i + 1) * GROUP, :], in_=q[:])
+
+        flip_w(0)
+        flip_x(0)
+        quantise_w(0)
+        flip_w(1)
+        quantise_x(0)
+        spread_bias()
+        for c in range(2, W_CHUNKS):
+            flip_w(c)
+            quantise_w(c - 1)
+        quantise_w(W_CHUNKS - 1)
+        flip_x(1)
+        for i in range(GROUPS):
+            for j in range(GROUP):
+                if j == GROUP // 2:
+                    if i + 1 < GROUPS:
+                        quantise_x(i + 1)
+                    if i + 2 < GROUPS:
+                        flip_x(i + 2)
+                multiply(i, j)
+
+        norms = const.tile([P, TILES], F32)
+        nc.scalar.activation(out=norms[:], in_=square_sums[:], func=ACT.Sqrt)
+        warm_exp = const.tile([P, 1], F32)
+        nc.scalar.activation(out=warm_exp[:], in_=norms[:, 0:1], func=ACT.Exp, scale=0.0)
+
+        by_user = sums.tile([P, CANDIDATES], F32, tag="sum")
+        for j in range(PER_USER):
+            nc.tensor.matmul(
+                out=by_user[:, j * TILES : (j + 1) * TILES],
+                lhsT=pick[:, j, :],
+                rhs=norms[:],
+                start=True,
+                stop=True,
+            )
+        minus_max = const.tile([P, 1], F32)
+        nc.vector.reduce_max(out=minus_max[:], in_=by_user[:], axis=AXIS.X, negate=True)
+        powers = const.tile([P, CANDIDATES], F32)
+        total = const.tile([P, 1], F32)
+        nc.scalar.activation(
+            out=powers[:],
+            in_=by_user[:],
+            func=ACT.Exp,
+            bias=minus_max[:, 0:1],
+            scale=1.0,
+            accum_out=total[:],
+        )
+        inverse = const.tile([P, 1], F32)
+        nc.vector.reciprocal(out=inverse[:], in_=total[:])
+        weights = const.tile([P, CANDIDATES], F32)
+        nc.vector.tensor_scalar_mul(out=weights[:], in0=powers[:], scalar1=inverse[:, 0:1])
+        nc.sync.dma_start(out=out_1, in_=weights[0:USERS, :])

@@ -14,9 +14,9 @@ AXIS = mybir.AxisListType
 
 P = 128
 PACK = 4
-USERS = 32
+USERS_IN_GROUP = 2
 CANDIDATES = 128
-ROWS = USERS * CANDIDATES
+ROWS = 32 * CANDIDATES
 K = 1024
 FEATURES = 1024
 PASSES = K // (P * PACK)
@@ -27,10 +27,11 @@ TILES = ROWS // P
 GROUP = 2
 GROUPS = TILES // GROUP
 VECTOR_SHARE = 4
+WARM_UP = 4
 W_BLOCKS = 2
 W_CHUNK = W_BLOCKS * P
 W_CHUNKS = FEATURES // W_CHUNK
-PER_USER = CANDIDATES // TILES
+PER_USER = P // USERS_IN_GROUP
 
 FLOPS = 2 * ROWS * K * FEATURES
 
@@ -39,8 +40,8 @@ def tile_candidateaware_clickednewsattention_pa_t_kernel(
     tc, cand_topics, Wq, bq, out_0, out_1
 ):
     nc = tc.nc
-    x_rows = cand_topics.flatten_outer_dims().rearrange("(p t) k -> p t k", t=TILES)
-    q_rows = out_0.flatten_outer_dims().rearrange("(p t) d -> p t d", t=TILES)
+    x_rows = cand_topics.flatten_outer_dims().rearrange("(i p j) k -> p i j k", p=P, j=GROUP)
+    q_rows = out_0.flatten_outer_dims().rearrange("(i p j) d -> p i j d", p=P, j=GROUP)
     w_rows = Wq.rearrange("(c p) k -> p c k", p=P)
 
     with ExitStack() as stack:
@@ -54,7 +55,11 @@ def tile_candidateaware_clickednewsattention_pa_t_kernel(
         stack.enter_context(tc.manual_schedule())
 
         bias_rows = const.tile([P, FEATURES], BF16)
-        nc.vector.memset(bias_rows[:], 0.0)
+        nc.gpsimd.memset(bias_rows[:], 0.0)
+        ones = const.tile([P, P], BF16)
+        nc.vector.memset(ones[:], 1.0)
+        zeros = const.tile([P, BANK], BF16)
+        nc.vector.memset(zeros[:], 0.0)
 
         w_raw = [
             raw.tile([P, W_BLOCKS, K], BF16, name="w_raw%d" % c) for c in range(W_CHUNKS)
@@ -67,7 +72,7 @@ def tile_candidateaware_clickednewsattention_pa_t_kernel(
             )
 
         def load_x(i):
-            nc.sync.dma_start(out=x_raw[i][:], in_=x_rows[:, i * GROUP : (i + 1) * GROUP, :])
+            nc.sync.dma_start(out=x_raw[i][:], in_=x_rows[:, i])
 
         load_w(0)
         load_x(0)
@@ -82,17 +87,14 @@ def tile_candidateaware_clickednewsattention_pa_t_kernel(
         warm_sqrt = const.tile([P, 1], F32)
         nc.scalar.activation(out=warm_sqrt[:], in_=one[:], func=ACT.Sqrt)
 
+        square_sums = const.tile([P, GROUPS, GROUP], F32)
+        rest_sum = const.tile([P, 1], F32)
+        norms = const.tile([P, GROUP, P], F32)
+        nc.vector.memset(norms[:], 0.0)
+
         ident = const.tile([P, P], F32)
         make_identity(nc, ident[:])
 
-        pick = const.tile([P, PER_USER, P], F32)
-        nc.vector.memset(pick[:], 0.0)
-        nc.vector.tensor_copy(
-            out=pick[:, :, 0:USERS], in_=ident[:].rearrange("p (b j) -> p j b", j=PER_USER)
-        )
-
-        ones = const.tile([P, P], BF16)
-        nc.vector.memset(ones[:], 1.0)
         bias = const.tile([P, FEATURES], F32)
 
         def spread_bias():
@@ -103,6 +105,13 @@ def tile_candidateaware_clickednewsattention_pa_t_kernel(
                     out=spread[:], lhsT=ones[:], rhs=bias_rows[:, cols], start=True, stop=True
                 )
                 nc.scalar.copy(out=bias[:, cols], in_=spread[:])
+
+        def warm(count):
+            unread = sums.tile([P, BANK], F32, tag="sum")
+            for n in range(count):
+                nc.tensor.matmul(
+                    out=unread[:], lhsT=ones[:], rhs=zeros[:], start=True, stop=True
+                )
 
         def flip(words, grouped_words, on_vector):
             bank = flipped.tile([P, BLOCKS, P], F32, tag="flip")
@@ -169,8 +178,6 @@ def tile_candidateaware_clickednewsattention_pa_t_kernel(
                 in_=x_grouped[i][:].rearrange("p j g r e -> p (j g r e)"),
             )
 
-        square_sums = const.tile([P, TILES], F32)
-
         q_group = {}
 
         def multiply(i, j):
@@ -195,24 +202,43 @@ def tile_candidateaware_clickednewsattention_pa_t_kernel(
                     out=q[:, j, cols], in0=acc[:], in1=bias[:, cols], op=ALU.add
                 )
             squares = scrap.tile([P, FEATURES], BF16, tag="squares")
+            is_last = t == TILES - 1
+            scalars_part = slice(0, BANK if is_last else FEATURES)
             nc.scalar.activation(
-                out=squares[:],
-                in_=q[:, j, :],
+                out=squares[:, scalars_part],
+                in_=q[:, j, scalars_part],
                 func=ACT.Square,
-                accum_out=square_sums[:, t : t + 1],
+                accum_out=square_sums[:, i, j : j + 1],
             )
-            if j == GROUP - 1:
-                nc.sync.dma_start(out=q_rows[:, i * GROUP : (i + 1) * GROUP, :], in_=q[:])
+            if is_last:
+                rest = slice(BANK, FEATURES)
+                nc.vector.scalar_tensor_tensor(
+                    out=squares[:, rest],
+                    in0=q[:, j, rest],
+                    scalar=1.0,
+                    in1=q[:, j, rest],
+                    op0=ALU.mult,
+                    op1=ALU.mult,
+                    accum_out=rest_sum[:],
+                )
+            if i == GROUPS - 1:
+                nc.sync.dma_start(out=q_rows[:, i, j], in_=q[:, j, :])
+            elif j == GROUP - 1:
+                nc.sync.dma_start(out=q_rows[:, i], in_=q[:])
 
+        warm(WARM_UP)
         flip_w(0)
+        warm(1)
         flip_x(0)
+        warm(1)
         quantise_w(0)
         flip_w(1)
         quantise_x(0)
-        spread_bias()
         for c in range(2, W_CHUNKS):
+            warm(1)
             flip_w(c)
             quantise_w(c - 1)
+        spread_bias()
         quantise_w(W_CHUNKS - 1)
         flip_x(1)
         for i in range(GROUPS):
@@ -224,34 +250,56 @@ def tile_candidateaware_clickednewsattention_pa_t_kernel(
                         flip_x(i + 2)
                 multiply(i, j)
 
-        norms = const.tile([P, TILES], F32)
-        nc.scalar.activation(out=norms[:], in_=square_sums[:], func=ACT.Sqrt)
-        warm_exp = const.tile([P, 1], F32)
-        nc.scalar.activation(out=warm_exp[:], in_=norms[:, 0:1], func=ACT.Exp, scale=0.0)
-
-        by_user = sums.tile([P, CANDIDATES], F32, tag="sum")
-        for j in range(PER_USER):
-            nc.tensor.matmul(
-                out=by_user[:, j * TILES : (j + 1) * TILES],
-                lhsT=pick[:, j, :],
-                rhs=norms[:],
-                start=True,
-                stop=True,
-            )
-        minus_max = const.tile([P, 1], F32)
-        nc.vector.reduce_max(out=minus_max[:], in_=by_user[:], axis=AXIS.X, negate=True)
-        powers = const.tile([P, CANDIDATES], F32)
-        total = const.tile([P, 1], F32)
+        early = slice(0, GROUPS - 1)
         nc.scalar.activation(
-            out=powers[:],
-            in_=by_user[:],
-            func=ACT.Exp,
-            bias=minus_max[:, 0:1],
-            scale=1.0,
-            accum_out=total[:],
+            out=norms[:, :, early].rearrange("p j i -> p i j"),
+            in_=square_sums[:, early, :],
+            func=ACT.Sqrt,
         )
-        inverse = const.tile([P, 1], F32)
-        nc.vector.reciprocal(out=inverse[:], in_=total[:])
-        weights = const.tile([P, CANDIDATES], F32)
-        nc.vector.tensor_scalar_mul(out=weights[:], in0=powers[:], scalar1=inverse[:, 0:1])
-        nc.sync.dma_start(out=out_1, in_=weights[0:USERS, :])
+        nc.scalar.activation(
+            out=norms[:, 0, GROUPS - 1 : GROUPS], in_=square_sums[:, GROUPS - 1, 0:1], func=ACT.Sqrt
+        )
+        nc.scalar.activation(
+            out=norms[:, 1, GROUPS - 1 : GROUPS],
+            in_=square_sums[:, GROUPS - 1, 1:2],
+            func=ACT.Sqrt,
+            bias=rest_sum[:],
+        )
+        warm_exp = const.tile([P, 1], F32)
+        nc.scalar.activation(out=warm_exp[:], in_=norms[:, 1, GROUPS - 1 : GROUPS], func=ACT.Exp, scale=0.0)
+        by_user = sums.tile([P, GROUP, USERS_IN_GROUP, PER_USER], F32, tag="sum")
+        for j in range(GROUP):
+            nc.tensor.transpose(
+                out=by_user[:, j].rearrange("p h m -> p (h m)"), in_=norms[:, j, :], identity=ident[:]
+            )
+        minus_max = const.tile([P, USERS_IN_GROUP], F32)
+        nc.vector.tensor_reduce(
+            out=minus_max[:],
+            in_=by_user[:].rearrange("p j h m -> p h j m"),
+            axis=AXIS.XY,
+            op=ALU.max,
+            negate=True,
+        )
+        powers = const.tile([P, USERS_IN_GROUP, GROUP, PER_USER], F32)
+        total = const.tile([P, USERS_IN_GROUP], F32)
+        for h in range(USERS_IN_GROUP):
+            nc.scalar.activation(
+                out=powers[:, h],
+                in_=by_user[:, :, h, :],
+                func=ACT.Exp,
+                bias=minus_max[:, h : h + 1],
+                scale=1.0,
+                accum_out=total[:, h : h + 1],
+            )
+        inverse = const.tile([P, USERS_IN_GROUP], F32)
+        weights = const.tile([P, USERS_IN_GROUP, CANDIDATES], F32)
+        for h in range(USERS_IN_GROUP):
+            nc.vector.reciprocal(out=inverse[:, h : h + 1], in_=total[:, h : h + 1])
+            nc.vector.tensor_scalar_mul(
+                out=weights[:, h].rearrange("p (m j) -> p j m", j=GROUP),
+                in0=powers[:, h],
+                scalar1=inverse[:, h : h + 1],
+            )
+        nc.sync.dma_start(
+            out=out_1.rearrange("(i h) n -> i h n", h=USERS_IN_GROUP), in_=weights[0:GROUPS]
+        )

from contextlib import ExitStack

import concourse.mybir as mybir
from concourse.masks import make_identity

F32 = mybir.dt.float32
BF16 = mybir.dt.bfloat16
U32 = mybir.dt.uint32
U8 = mybir.dt.uint8
FP8X4 = mybir.dt.float8_e4m3fn_x4
ACT = mybir.ActivationFunctionType
ALU = mybir.AluOpType
AXIS = mybir.AxisListType

P = 128
PACK = 4
USERS_IN_GROUP = 2
CANDIDATES = 128
ROWS = 32 * CANDIDATES
K = 1024
FEATURES = 1024
PASSES = K // (P * PACK)
BLOCKS = K // 2 // P
BANK = 512
HALVES = FEATURES // BANK
TILES = ROWS // P
GROUP = 2
GROUPS = TILES // GROUP
VECTOR_SHARE = 4
WARM_UP = 4
W_BLOCKS = 2
W_CHUNK = W_BLOCKS * P
W_CHUNKS = FEATURES // W_CHUNK
PER_USER = P // USERS_IN_GROUP

FLOPS = 2 * ROWS * K * FEATURES


def tile_candidateaware_clickednewsattention_pa_t_kernel(
    tc, cand_topics, Wq, bq, out_0, out_1
):
    nc = tc.nc
    x_rows = cand_topics.flatten_outer_dims().rearrange("(i p j) k -> p i j k", p=P, j=GROUP)
    q_rows = out_0.flatten_outer_dims().rearrange("(i p j) d -> p i j d", p=P, j=GROUP)
    w_rows = Wq.rearrange("(c p) k -> p c k", p=P)

    with ExitStack() as stack:
        const = stack.enter_context(tc.tile_pool(name="const", bufs=1))
        raw = stack.enter_context(tc.tile_pool(name="raw", bufs=1))
        packed = stack.enter_context(tc.tile_pool(name="packed", bufs=2))
        results = stack.enter_context(tc.tile_pool(name="results", bufs=6))
        scrap = stack.enter_context(tc.tile_pool(name="scrap", bufs=4))
        flipped = stack.enter_context(tc.psum_pool(name="flipped", bufs=4))
        sums = stack.enter_context(tc.psum_pool(name="sums", bufs=4))
        stack.enter_context(tc.manual_schedule())

        bias_rows = const.tile([P, FEATURES], BF16)
        nc.gpsimd.memset(bias_rows[:], 0.0)
        ones = const.tile([P, P], BF16)
        nc.vector.memset(ones[:], 1.0)
        zeros = const.tile([P, BANK], BF16)
        nc.vector.memset(zeros[:], 0.0)

        w_raw = [
            raw.tile([P, W_BLOCKS, K], BF16, name="w_raw%d" % c) for c in range(W_CHUNKS)
        ]
        x_raw = [raw.tile([P, GROUP, K], BF16, name="x_raw%d" % i) for i in range(GROUPS)]

        def load_w(c):
            nc.sync.dma_start(
                out=w_raw[c][:], in_=w_rows[:, c * W_BLOCKS : (c + 1) * W_BLOCKS, :]
            )

        def load_x(i):
            nc.sync.dma_start(out=x_raw[i][:], in_=x_rows[:, i])

        load_w(0)
        load_x(0)
        nc.sync.dma_start(out=bias_rows[0:1, :], in_=bq.unsqueeze(0))
        for c in range(1, W_CHUNKS):
            load_w(c)
        for i in range(1, GROUPS):
            load_x(i)

        one = const.tile([P, 1], F32)
        nc.vector.memset(one[:], 1.0)
        warm_sqrt = const.tile([P, 1], F32)
        nc.scalar.activation(out=warm_sqrt[:], in_=one[:], func=ACT.Sqrt)

        square_sums = const.tile([P, GROUPS, GROUP], F32)
        rest_sum = const.tile([P, 1], F32)
        norms = const.tile([P, GROUP, P], F32)
        nc.vector.memset(norms[:], 0.0)

        ident = const.tile([P, P], F32)
        make_identity(nc, ident[:])

        bias = const.tile([P, FEATURES], F32)

        def spread_bias():
            for h in range(HALVES):
                cols = slice(h * BANK, (h + 1) * BANK)
                spread = sums.tile([P, BANK], F32, tag="sum")
                nc.tensor.matmul(
                    out=spread[:], lhsT=ones[:], rhs=bias_rows[:, cols], start=True, stop=True
                )
                nc.scalar.copy(out=bias[:, cols], in_=spread[:])

        def warm(count):
            unread = sums.tile([P, BANK], F32, tag="sum")
            for n in range(count):
                nc.tensor.matmul(
                    out=unread[:], lhsT=ones[:], rhs=zeros[:], start=True, stop=True
                )

        def flip(words, grouped_words, on_vector):
            bank = flipped.tile([P, BLOCKS, P], F32, tag="flip")
            for g in range(PASSES):
                for u in range(2):
                    nc.tensor.transpose(
                        out=bank[:, 2 * g + u, :],
                        in_=words[:, 2 * P * g + u : 2 * P * (g + 1) : 2],
                        identity=ident[:],
                    )
            planes = bank[:].rearrange("p (g u) r -> p g r u", u=2)
            if on_vector:
                nc.vector.tensor_copy(out=grouped_words, in_=planes)
            else:
                nc.scalar.copy(out=grouped_words, in_=planes)

        w_grouped = const.tile([P, PASSES, FEATURES, PACK], BF16, align_bytes=64)
        w_codes = const.tile([P, PASSES, FEATURES], U32, align_bytes=64)
        w_scales = const.tile([P, PASSES, FEATURES], U8, align_bytes=64)

        def flip_w(c):
            for b in range(W_BLOCKS):
                first = c * W_CHUNK + b * P
                flip(
                    w_raw[c][:].bitcast(F32)[:, b, :],
                    w_grouped[:].bitcast(F32)[:, :, first : first + P, :],
                    on_vector=(b == 0),
                )

        def quantise_w(c):
            cols = slice(c * W_CHUNK, (c + 1) * W_CHUNK)
            for g in range(PASSES):
                nc.vector.quantize_mx(
                    out=w_codes[:, g, cols].bitcast(FP8X4),
                    scales=w_scales[:, g, cols],
                    in_=w_grouped[:, g, cols, :].rearrange("p d e -> p (d e)"),
                )

        x_grouped = {}
        x_codes = {}
        x_scales = {}

        def flip_x(i):
            x_grouped[i] = packed.tile(
                [P, GROUP, PASSES, P, PACK], BF16, align_bytes=64, name="x_grouped", tag="xg"
            )
            for j in range(GROUP):
                flip(
                    x_raw[i][:].bitcast(F32)[:, j, :],
                    x_grouped[i][:].bitcast(F32)[:, j],
                    on_vector=((i * GROUP + j) % VECTOR_SHARE == 0),
                )

        def quantise_x(i):
            x_codes[i] = packed.tile(
                [P, GROUP, PASSES, P], U32, align_bytes=64, name="x_codes", tag="xc"
            )
            x_scales[i] = packed.tile(
                [P, GROUP, PASSES, P], U8, align_bytes=64, name="x_scales", tag="xs"
            )
            nc.vector.quantize_mx(
                out=x_codes[i][:].rearrange("p j g r -> p (j g r)").bitcast(FP8X4),
                scales=x_scales[i][:].rearrange("p j g r -> p (j g r)"),
                in_=x_grouped[i][:].rearrange("p j g r e -> p (j g r e)"),
            )

        q_group = {}

        def multiply(i, j):
            t = i * GROUP + j
            if j == 0:
                q_group[i] = results.tile([P, GROUP, FEATURES], F32, name="q", tag="q")
            q = q_group[i]
            for h in range(HALVES):
                cols = slice(h * BANK, (h + 1) * BANK)
                acc = sums.tile([P, BANK], F32, tag="sum")
                for g in range(PASSES):
                    nc.tensor.matmul_mx(
                        out=acc[:],
                        lhsT=x_codes[i][:, j, g, :].bitcast(FP8X4),
                        lhsT_scale=x_scales[i][:, j, g, :],
                        rhs=w_codes[:, g, cols].bitcast(FP8X4),
                        rhs_scale=w_scales[:, g, cols],
                        start=(g == 0),
                        stop=(g == PASSES - 1),
                    )
                nc.vector.tensor_tensor(
                    out=q[:, j, cols], in0=acc[:], in1=bias[:, cols], op=ALU.add
                )
            squares = scrap.tile([P, FEATURES], BF16, tag="squares")
            is_last = t == TILES - 1
            scalars_part = slice(0, BANK if is_last else FEATURES)
            nc.scalar.activation(
                out=squares[:, scalars_part],
                in_=q[:, j, scalars_part],
                func=ACT.Square,
                accum_out=square_sums[:, i, j : j + 1],
            )
            if is_last:
                rest = slice(BANK, FEATURES)
                nc.vector.scalar_tensor_tensor(
                    out=squares[:, rest],
                    in0=q[:, j, rest],
                    scalar=1.0,
                    in1=q[:, j, rest],
                    op0=ALU.mult,
                    op1=ALU.mult,
                    accum_out=rest_sum[:],
                )
            if i == GROUPS - 1:
                nc.sync.dma_start(out=q_rows[:, i, j], in_=q[:, j, :])
            elif j == GROUP - 1:
                nc.sync.dma_start(out=q_rows[:, i], in_=q[:])

        warm(WARM_UP)
        flip_w(0)
        warm(1)
        flip_x(0)
        warm(1)
        quantise_w(0)
        flip_w(1)
        quantise_x(0)
        for c in range(2, W_CHUNKS):
            warm(1)
            flip_w(c)
            quantise_w(c - 1)
        spread_bias()
        quantise_w(W_CHUNKS - 1)
        flip_x(1)
        for i in range(GROUPS):
            for j in range(GROUP):
                if j == GROUP // 2:
                    if i + 1 < GROUPS:
                        quantise_x(i + 1)
                    if i + 2 < GROUPS:
                        flip_x(i + 2)
                multiply(i, j)

        early = slice(0, GROUPS - 1)
        nc.scalar.activation(
            out=norms[:, :, early].rearrange("p j i -> p i j"),
            in_=square_sums[:, early, :],
            func=ACT.Sqrt,
        )
        nc.scalar.activation(
            out=norms[:, 0, GROUPS - 1 : GROUPS], in_=square_sums[:, GROUPS - 1, 0:1], func=ACT.Sqrt
        )
        nc.scalar.activation(
            out=norms[:, 1, GROUPS - 1 : GROUPS],
            in_=square_sums[:, GROUPS - 1, 1:2],
            func=ACT.Sqrt,
            bias=rest_sum[:],
        )
        warm_exp = const.tile([P, 1], F32)
        nc.scalar.activation(out=warm_exp[:], in_=norms[:, 1, GROUPS - 1 : GROUPS], func=ACT.Exp, scale=0.0)
        by_user = sums.tile([P, GROUP, USERS_IN_GROUP, PER_USER], F32, tag="sum")
        for j in range(GROUP):
            nc.tensor.transpose(
                out=by_user[:, j].rearrange("p h m -> p (h m)"), in_=norms[:, j, :], identity=ident[:]
            )
        minus_max = const.tile([P, USERS_IN_GROUP], F32)
        nc.vector.tensor_reduce(
            out=minus_max[:],
            in_=by_user[:].rearrange("p j h m -> p h j m"),
            axis=AXIS.XY,
            op=ALU.max,
            negate=True,
        )
        powers = const.tile([P, USERS_IN_GROUP, GROUP, PER_USER], F32)
        total = const.tile([P, USERS_IN_GROUP], F32)
        for h in range(USERS_IN_GROUP):
            nc.scalar.activation(
                out=powers[:, h],
                in_=by_user[:, :, h, :],
                func=ACT.Exp,
                bias=minus_max[:, h : h + 1],
                scale=1.0,
                accum_out=total[:, h : h + 1],
            )
        inverse = const.tile([P, USERS_IN_GROUP], F32)
        weights = const.tile([P, USERS_IN_GROUP, CANDIDATES], F32)
        for h in range(USERS_IN_GROUP):
            nc.vector.reciprocal(out=inverse[:, h : h + 1], in_=total[:, h : h + 1])
            nc.vector.tensor_scalar_mul(
                out=weights[:, h].rearrange("p (m j) -> p j m", j=GROUP),
                in0=powers[:, h],
                scalar1=inverse[:, h : h + 1],
            )
        nc.sync.dma_start(
            out=out_1.rearrange("(i h) n -> i h n", h=USERS_IN_GROUP), in_=weights[0:GROUPS]
        )
